import numpy as np
import ml_dtypes


BF16 = ml_dtypes.bfloat16


def bf(x):
    return np.asarray(x, np.float32).astype(BF16)


def f64(x):
    return np.asarray(x).astype(np.float64)


E2M1 = np.array([0.0, 0.5, 1.0, 1.5, 2.0, 3.0, 4.0, 6.0, -0.0, -0.5, -1.0, -1.5, -2.0, -3.0, -4.0, -6.0])


def pack_weight(w, fmt):
    k, n = w.shape
    w = f64(bf(w)).reshape(k // 32, 32, n)
    amax = np.abs(w).max(1)
    if fmt == "e4m3":
        byte = np.frexp(amax)[1] - 1 + 127 - 7
    else:
        mant, ex = np.frexp(amax / 6.0)
        byte = np.where(mant > 0.5, ex, ex - 1) + 127
    byte = np.clip(np.where(amax > 0, byte, 1), 1, 254)
    scaled = (w * np.exp2(127.0 - byte)[:, None, :]).reshape(k, n).astype(np.float32)
    by_word = np.ascontiguousarray(scaled.reshape(k // 512, 128, 4, n).transpose(0, 1, 3, 2))
    if fmt == "e4m3":
        words = by_word.astype(ml_dtypes.float8_e4m3fn).view(np.uint8)
    else:
        c = by_word.astype(ml_dtypes.float4_e2m1fn).view(np.uint8) & 0xF
        words = c[..., 0::2] | (c[..., 1::2] << 4)
    return np.ascontiguousarray(words), np.ascontiguousarray(byte.astype(np.uint8).reshape(k // 512, 16, n))


def unpack_weight(words, scales, fmt):
    g, p, n, _ = words.shape
    if fmt == "e4m3":
        vals = np.ascontiguousarray(words).view(ml_dtypes.float8_e4m3fn).astype(np.float64)
    else:
        nib = np.empty((g, p, n, 4), np.uint8)
        nib[..., 0::2] = words & 0xF
        nib[..., 1::2] = words >> 4
        vals = E2M1[nib]
    vals = vals * np.repeat(np.exp2(scales.astype(np.float64) - 127.0), 8, axis=1)[..., None]
    return vals.transpose(0, 1, 3, 2).reshape(g * 512, n)

def pack4(w):
    words, scales = pack_weight(w, "e2m1")
    return words.reshape(words.shape[0], 128, -1), scales


def unpack4(words, scales):
    return unpack_weight(words.reshape(words.shape[0], 128, -1, 2), scales, "e2m1")


def kspread(k):
    return np.exp2(np.repeat(np.random.randint(-6, 7, k // 32), 32).astype(np.float64))


B, HH, WW, C, NH, DIM = 2, 16, 32, 4096, 8, 128
N = HH * WW
HD = NH * DIM
F = 4 * HD
BN_EPS = 1e-5
WS = 0.02
GQK = np.sqrt(2.8) / DIM ** 0.25
GV = 4.0


def heads(t):
    return t.reshape(B, N, NH, DIM).transpose(0, 2, 1, 3)


def setup_inputs():
    s = kspread(C)
    x = np.random.standard_normal((B, HH, WW, C)) + 0.5 * np.random.standard_normal(C)
    gain = np.concatenate([np.full(2 * HD, GQK), np.full(2 * HD, GV)])
    inputs_words, inputs_scales = pack4((x * s).reshape(B * N, C).T)
    words, scales = pack4(np.random.standard_normal((C, F)) * WS / np.sqrt(C) / s[:, None])
    return {"inputs_words": inputs_words,
            "inputs_scales": inputs_scales,
            "w_qkv_words": words,
            "w_qkv_scales": scales,
            "bn_scale": bf(np.random.standard_normal(F) * gain)}


def reference(inputs_words, inputs_scales, w_qkv_words, w_qkv_scales, bn_scale):
    x = unpack4(inputs_words, inputs_scales).T @ unpack4(w_qkv_words, w_qkv_scales)
    mean = x.mean(axis=0)
    var = x.var(axis=0)
    x = (x - mean) / np.sqrt(var + BN_EPS) * f64(bn_scale)
    q, k, v1, v2 = (heads(t) for t in np.split(x.reshape(B, N, F), 4, axis=-1))
    v = np.concatenate((v1, v2), axis=-1)
    return np.ascontiguousarray(q), np.ascontiguousarray(k), v

@@ -1,0 +1,411 @@
+from contextlib import ExitStack
+
+import concourse.mybir as mybir
+from concourse.masks import make_identity
+
+F32 = mybir.dt.float32
+BF16 = mybir.dt.bfloat16
+U8 = mybir.dt.uint8
+I32 = mybir.dt.int32
+FP4 = mybir.dt.float4_e2m1fn_x4
+ACT = mybir.ActivationFunctionType
+ALU = mybir.AluOpType
+
+P = 128
+G = 8
+MAPS = 2
+PIX = 512
+EPS = 1e-5
+FLOPS = 2 * 1024 * 4096 * 4096
+
+UNITS = [4, 5, 6, 7, 0, 1, 2]
+SPECIAL = 3
+GROUPS = [[4], [5], [6, 7], [0, 1], [2, 3]]
+
+
+def tile_levitattention_pa_kernel(tc, inputs_words, inputs_scales, w_qkv_words, w_qkv_scales, bn_scale, out_0, out_1, out_2):
+    nc = tc.nc
+    with ExitStack() as ctx:
+        keep = ctx.enter_context(tc.tile_pool(name="keep", bufs=1))
+        work = ctx.enter_context(tc.tile_pool(name="work", bufs=1))
+        psum = ctx.enter_context(tc.psum_pool(name="psum", bufs=8))
+
+        ident_f = keep.tile([P, P], F32, name="ident_f")
+        make_identity(nc, ident_f[:])
+        ident_b = keep.tile([P, P], BF16, name="ident_b")
+        make_identity(nc, ident_b[:])
+
+        ctx.enter_context(tc.manual_schedule())
+
+        def words(ap):
+            return ap.bitcast(I32)
+
+        def load_scales(dst, src):
+            for q in range(4):
+                nc.sync.dma_start(
+                    out=words(dst[32 * q : 32 * q + 4, :, :]),
+                    in_=words(src[:, 4 * q : 4 * q + 4, :].rearrange("g r n -> r g n")),
+                )
+
+        def load_codes(dst, src):
+            nc.sync.dma_start(out=words(dst[:, :, :]), in_=words(src.rearrange("g p n -> p g n")))
+
+        warm = keep.tile([P, PIX], BF16, name="warm")
+        nc.gpsimd.memset(warm[:], 0.0)
+        gain_rows = keep.tile([P, P], BF16, name="gain_rows")
+        nc.gpsimd.memset(gain_rows[:], 0.0)
+
+        first = UNITS[0]
+        ws_raw = {}
+        wc_raw = {}
+        ws0 = keep.tile([P, G, 512], U8, name="ws0", align_bytes=64)
+        nc.vector.memset(ws0[:].bitcast(I32), 0)
+        xs_a = keep.tile([P, 2, 1024], U8, name="xs_a", align_bytes=64)
+        nc.vector.memset(xs_a[:].bitcast(I32), 0)
+        xs_b = keep.tile([P, 6, 1024], U8, name="xs_b", align_bytes=64)
+        nc.vector.memset(xs_b[:].bitcast(I32), 0)
+
+        chunk_of = []
+        chunks = [(0, 1), (1, 2), (2, 4), (4, 8)]
+        wc0 = []
+        xc = []
+        for c, (a, b) in enumerate(chunks):
+            wt = keep.tile([P, b - a, 1024], U8, name=f"wc0_{c}", align_bytes=64)
+            xt_ = keep.tile([P, b - a, 2048], U8, name=f"xc_{c}", align_bytes=64)
+            wc0.append(wt)
+            xc.append(xt_)
+            for g in range(a, b):
+                chunk_of.append((c, g - a))
+
+        def load_w0(c):
+            a, b = chunks[c]
+            load_codes(wc0[c], w_qkv_words[a:b, :, 1024 * first : 1024 * first + 1024])
+
+        def load_x(c):
+            a, b = chunks[c]
+            load_codes(xc[c], inputs_words[a:b, :, :])
+
+        load_w0(0)
+        load_x(0)
+        load_scales(ws0, w_qkv_scales[:, :, 512 * first : 512 * first + 512])
+        load_scales(xs_a, inputs_scales[0:2])
+        load_w0(1)
+        load_x(1)
+        load_scales(xs_b, inputs_scales[2:8])
+        load_w0(2)
+        load_x(2)
+        load_w0(3)
+        load_x(3)
+
+        by_tile = bn_scale.rearrange("(v q i c) -> i v q c", v=8, q=4, i=4)
+        for i in range(4):
+            nc.gpsimd.dma_start(
+                out=gain_rows[8 * i : 8 * i + 8, :].rearrange("v (q c) -> v q c", q=4), in_=by_tile[i]
+            )
+        pair = bn_scale[1536:1792].rearrange("(one h s i c) -> i one s h c", one=1, h=2, s=2, i=2)
+        for i in range(2):
+            nc.gpsimd.dma_start(
+                out=gain_rows[32 + i : 33 + i, :].rearrange("v (s h c) -> v s h c", s=2, h=2), in_=pair[i]
+            )
+        nc.gpsimd.dma_start(out=gain_rows[34:36, :], in_=bn_scale[1792:2048].rearrange("(n d) -> n d", n=2))
+
+        acc_w = psum.tile([P, PIX], F32, name="acc")
+        for _ in range(7):
+            nc.tensor.matmul(acc_w[:], warm[:, 0:P], warm[:], start=True, stop=True)
+
+        pc0 = []
+
+        def permute_w0(c):
+            a, b = chunks[c]
+            t = keep.tile([P, b - a, 4, 256], U8, name=f"pc0_{c}", align_bytes=64)
+            for g in range(b - a):
+                nc.vector.tensor_copy(
+                    out=t[:, g].rearrange("p i n -> p (i n)").bitcast(I32).rearrange("p (i q w) -> p i q w", i=4, q=4),
+                    in_=wc0[c][:, g].bitcast(I32).rearrange("p (q i w) -> p i q w", q=4, i=4),
+                )
+            pc0.append(t)
+
+        ring_s = {}
+        ring_c = {}
+
+        def permute_scales(n, raw, i):
+            t = work.tile([P, G, P], U8, name="perm_s", bufs=6, align_bytes=64)
+            nc.vector.tensor_copy(
+                out=t[:].bitcast(I32).rearrange("p g (q w) -> p g q w", q=4),
+                in_=raw.bitcast(I32).rearrange("p g (q i w) -> p i g q w", q=4, i=4)[:, i],
+            )
+            ring_s[n] = t
+
+        permute_w0(0)
+        for i in range(4):
+            permute_scales(i, ws0[:], i)
+        permute_w0(1)
+
+        wg_c = {}
+        wg_s = {}
+
+        def zero_group(k):
+            vs = GROUPS[k]
+            s = keep.tile([P, G, 512 * len(vs)], U8, name=f"wg_s{k}", align_bytes=64)
+            nc.vector.memset(s[:].bitcast(I32), 0)
+            return s
+
+        def load_group(k, s):
+            vs = GROUPS[k]
+            n = len(vs)
+            c = keep.tile([P, G, 1024 * n], U8, name=f"wg_c{k}", align_bytes=64)
+            lo = vs[0]
+            load_scales(s, w_qkv_scales[:, :, 512 * lo : 512 * (lo + n)])
+            load_codes(c, w_qkv_words[:, :, 1024 * lo : 1024 * (lo + n)])
+            for x, v in enumerate(vs):
+                wc_raw[v] = c[:, :, 1024 * x : 1024 * x + 1024]
+                ws_raw[v] = s[:, :, 512 * x : 512 * x + 512]
+
+        permute_w0(2)
+        s1 = zero_group(1)
+        load_group(1, s1)
+        permute_w0(3)
+        for k in (2, 3, 4):
+            sk = zero_group(k)
+            load_group(k, sk)
+
+        def permute(n):
+            t = work.tile([P, G, 256], U8, name="perm_c", bufs=4, align_bytes=64)
+            out = t[:].bitcast(I32).rearrange("p g (q w) -> p g q w", q=4)
+            if n < 28:
+                v, i = UNITS[n // 4], n % 4
+                nc.vector.tensor_copy(
+                    out=out, in_=wc_raw[v].bitcast(I32).rearrange("p g (q i w) -> p i g q w", q=4, i=4)[:, i]
+                )
+                permute_scales(n, ws_raw[v], i)
+            else:
+                i = n - 28
+                s = work.tile([P, G, P], U8, name="perm_s", bufs=6, align_bytes=64)
+                out_s = s[:].bitcast(I32).rearrange("p g (q w) -> p g q w", q=4)
+                raw_c = wc_raw[SPECIAL][:, :, 0:512].bitcast(I32).rearrange("p g (h s i w) -> p i s g h w", h=2, s=2, i=2)
+                raw_s = ws_raw[SPECIAL][:, :, 0:256].bitcast(I32).rearrange("p g (h s i w) -> p i s g h w", h=2, s=2, i=2)
+                for half in range(2):
+                    nc.vector.tensor_copy(out=out[:, :, 2 * half : 2 * half + 2], in_=raw_c[:, i, half])
+                    nc.vector.tensor_copy(out=out_s[:, :, 2 * half : 2 * half + 2], in_=raw_s[:, i, half])
+                ring_s[n] = s
+            ring_c[n] = t
+
+        acc = {}
+
+        def one_pass(n, m, g, lo=0, hi=PIX):
+            if (n, m) not in acc:
+                acc[(n, m)] = psum.tile([P, PIX], F32, name="acc")
+            if n < 4:
+                c, k = chunk_of[g]
+                w_c = pc0[c][:, k, n, :]
+                w_s = ring_s[n][:, g, :]
+            elif n < 30:
+                w_c = ring_c[n][:, g, :]
+                w_s = ring_s[n][:, g, :]
+            else:
+                h = n - 28
+                w_c = wc_raw[SPECIAL][:, g, 256 * h : 256 * h + 256]
+                w_s = ws_raw[SPECIAL][:, g, 128 * h : 128 * h + 128]
+            c, k = chunk_of[g]
+            x_s = xs_a[:, g] if g < 2 else xs_b[:, g - 2]
+            nc.tensor.matmul_mx(
+                out=acc[(n, m)][:, lo:hi],
+                lhsT=w_c.bitcast(FP4),
+                lhsT_scale=w_s,
+                rhs=xc[c][:, k, 1024 * m + 2 * lo : 1024 * m + 2 * hi].bitcast(FP4),
+                rhs_scale=x_s[:, PIX * m + lo : PIX * m + hi],
+                start=(g == 0),
+                stop=(g == G - 1),
+            )
+
+        stat = {}
+
+        def stats(n, m, lo=0, hi=PIX, slot=None):
+            if n not in stat:
+                stat[n] = work.tile([P, 3, 6], F32, name="stat", bufs=3)
+            k = m if slot is None else slot
+            nc.vector.bn_stats(out=stat[n][:, k, :], in_=acc[(n, m)][:, lo:hi])
+
+        gain = keep.tile([P, 36], F32, name="gain")
+        coef = {}
+
+        def aggregate(n, parts=2):
+            mv = work.tile([P, 2], F32, name="mv", bufs=3)
+            nc.vector.bn_aggr(out=mv[:], in_=stat[n][:, 0:parts, :].rearrange("p a b -> p (a b)"))
+            rstd = work.tile([P, 1], F32, name="rstd", bufs=3)
+            nc.scalar.activation(out=rstd[:], in_=mv[:, 1:2], func=ACT.Abs_reciprocal_sqrt, bias=EPS, scale=1.0)
+            coef[n] = (mv, rstd)
+
+        def factors(n):
+            mv, rstd = coef[n]
+            col = 8 * (n % 4) + UNITS[n // 4] if n < 28 else 32 + n - 28
+            scale = work.tile([P, 1], F32, name="scale", bufs=3)
+            shift = work.tile([P, 1], F32, name="shift", bufs=3)
+            nc.vector.tensor_mul(out=scale[:], in0=rstd[:], in1=gain[:, col : col + 1])
+            nc.vector.scalar_tensor_tensor(
+                out=shift[:], in0=mv[:, 0:1], scalar=-1.0, in1=scale[:], op0=ALU.mult, op1=ALU.mult
+            )
+            coef[n] = (scale, shift)
+
+        xn = {}
+
+        def normalise(n):
+            scale, shift = coef[n]
+            for m in range(MAPS):
+                if n < 30:
+                    u = n // 4
+                    tiles = 4 if n < 28 else 2
+                    if (u, m) not in xn:
+                        xn[(u, m)] = work.tile([P, 16, tiles, 32], F32, name="xn", bufs=4, align_bytes=64)
+                    dst = xn[(u, m)][:, :, n % 4, :]
+                    src = acc[(n, m)][:].rearrange("p (t j) -> p j t", j=16)
+                else:
+                    xn[(n, m)] = work.tile([P, 4, P], F32, name="xnat", bufs=4, align_bytes=64)
+                    dst = xn[(n, m)][:]
+                    src = acc[(n, m)][:].rearrange("p (t j) -> p j t", j=4)
+                nc.scalar.activation(out=dst, in_=src, func=ACT.Identity, bias=shift[:], scale=scale[:])
+
+        xt = {}
+
+        def turn(u, m, half):
+            tiles = 4 if u < 7 else 2
+            if (u, m) not in xt:
+                xt[(u, m)] = work.tile([P, 16, tiles, 32], F32, name="xt", bufs=4, align_bytes=64)
+            lo, hi = (8 * half, 8 * half + 8) if half is not None else (0, 16)
+            nc.vector.transpose(
+                out=xt[(u, m)][:, lo:hi].rearrange("p j i c -> p (j i c)"),
+                in_=xn[(u, m)][:, lo:hi].rearrange("p j i t -> p (j i t)"),
+            )
+
+        def store(u, m):
+            src = xt[(u, m)][:].rearrange("p j i c -> p j (i c)")
+            if u < 7:
+                v = UNITS[u]
+                quarter, h0 = v // 2, 4 * (v % 2)
+                if quarter == 0:
+                    dst = out_0[m, h0 : h0 + 4]
+                elif quarter == 1:
+                    dst = out_1[m, h0 : h0 + 4]
+                else:
+                    dst = out_2[m, h0 : h0 + 4, :, P * (quarter - 2) : P * (quarter - 1)]
+                nc.sync.dma_start(out=dst.rearrange("h (t j) d -> (h t) j d", j=16), in_=src)
+            else:
+                for s in range(2):
+                    nc.sync.dma_start(
+                        out=out_1[m, 4:6, :, 64 * s : 64 * s + 64].rearrange("h (t j) d -> (h t) j d", j=16),
+                        in_=src[64 * s : 64 * s + 64],
+                    )
+
+        for g in range(G):
+            for m in range(MAPS):
+                for n in range(3):
+                    one_pass(n, m, g)
+
+        gain_p = psum.tile([P, P], BF16, name="acc")
+        nc.tensor.transpose(gain_p[:], gain_rows[:], ident_b[:])
+        nc.vector.tensor_copy(out=gain[:], in_=gain_p[:, 0:36])
+
+        pieces = []
+
+        def finish(n, between=None):
+            aggregate(n)
+            if between is not None:
+                permute(between)
+            factors(n)
+            normalise(n)
+            if n % 4 == 3 and n < 28:
+                for m in range(MAPS):
+                    for half in range(2):
+                        pieces.append((n // 4, m, half))
+
+        def next_piece():
+            if pieces:
+                u, m, half = pieces.pop(0)
+                turn(u, m, half)
+                if half == 1:
+                    store(u, m)
+
+        for g in range(G):
+            one_pass(3, 0, g)
+        for g in range(G):
+            one_pass(3, 1, g)
+        for n in range(3):
+            stats(n, 0)
+            stats(n, 1)
+            finish(n, between=4 + n if n < 2 else None)
+        stats(3, 0)
+
+        for n in range(4, 31):
+            stats(n - 1, 1)
+            if n - 1 >= 4 or n == 4:
+                ready = 0 if n == 4 else len(pieces)
+            finish(n - 1, between=n + 2 if n + 2 < 30 else None)
+            if ready:
+                next_piece()
+                if n >= 29:
+                    next_piece()
+            for g in range(G):
+                one_pass(n, 0, g)
+            stats(n, 0)
+            for g in range(G):
+                one_pass(n, 1, g)
+            if n == 30:
+                turn(7, 0, None)
+                store(7, 0)
+
+        stats(30, 1)
+        finish(30)
+        turn(7, 1, None)
+        store(7, 1)
+        for g in range(G):
+            one_pass(31, 0, g)
+        stats(31, 0)
+        for part in range(2):
+            lo = 256 * part
+            for g in range(G):
+                one_pass(31, 1, g, lo, lo + 256)
+            stats(31, 1, lo, lo + 256, slot=1 + part)
+
+        def turn_natural(n, m, lo, hi, bank):
+            for j in range(lo, hi):
+                nc.tensor.transpose(bank[:, P * j : P * j + P], xn[(n, m)][:, j, :], ident_f[:])
+
+        res = {}
+        for m in range(MAPS):
+            bank = psum.tile([P, PIX], F32, name="acc")
+            turn_natural(30, m, 0, 4, bank)
+            res[m] = work.tile([P, 4, P], F32, name="res", bufs=4, align_bytes=64)
+            acc[(30, m)] = bank
+        nc.scalar.copy(out=res[0][:].rearrange("p j d -> p (j d)"), in_=acc[(30, 0)][:])
+        aggregate(31, parts=3)
+        nc.vector.tensor_copy(out=res[1][:].rearrange("p j d -> p (j d)"), in_=acc[(30, 1)][:])
+        for m in range(MAPS):
+            nc.sync.dma_start(out=out_1[m, 6].rearrange("(t j) d -> t j d", j=4), in_=res[m][:])
+        factors(31)
+        scale, shift = coef[31]
+        xl = []
+        banks = []
+        last = []
+        for m in range(MAPS):
+            t = work.tile([P, 4, P], F32, name="xnat", bufs=4, align_bytes=64)
+            xl.append(t)
+            xn[(31, m)] = t
+            r = work.tile([P, 4, P], F32, name="res", bufs=4, align_bytes=64)
+            last.append(r)
+        for half in range(2):
+            a, b = 2 * half, 2 * half + 2
+            src = [acc[(31, m)][:].rearrange("p (t j) -> p j t", j=4)[:, a:b, :] for m in range(MAPS)]
+            nc.scalar.activation(out=xl[0][:, a:b, :], in_=src[0], func=ACT.Identity, bias=shift[:], scale=scale[:])
+            nc.vector.tensor_scalar(
+                out=xl[1][:, a:b, :], in0=src[1], scalar1=scale[:], scalar2=shift[:], op0=ALU.mult, op1=ALU.add
+            )
+        for m in range(MAPS):
+            bank = psum.tile([P, PIX], F32, name="acc")
+            banks.append(bank)
+        for half in range(2):
+            for m in range(MAPS):
+                turn_natural(31, m, 2 * half, 2 * half + 2, banks[m])
+        nc.scalar.copy(out=last[0][:].rearrange("p j d -> p (j d)"), in_=banks[0][:])
+        nc.vector.tensor_copy(out=last[1][:].rearrange("p j d -> p (j d)"), in_=banks[1][:])
+        nc.scalar.dma_start(out=out_1[0, 7].rearrange("(t j) d -> t j d", j=4), in_=last[0][:])
+        nc.sync.dma_start(out=out_1[1, 7].rearrange("(t j) d -> t j d", j=4), in_=last[1][:])

@@ -16,6 +16,7 @@ G = 8
 MAPS = 2
 PIX = 512
 EPS = 1e-5
+SA = 3
 FLOPS = 2 * 1024 * 4096 * 4096
 
 UNITS = [4, 5, 6, 7, 0, 1, 2]
@@ -58,11 +59,13 @@ def tile_levitattention_pa_kernel(tc, inputs_words, inputs_scales, w_qkv_words, 
         first = UNITS[0]
         ws_raw = {}
         wc_raw = {}
-        ws0 = keep.tile([P, G, 512], U8, name="ws0", align_bytes=64)
-        nc.vector.memset(ws0[:].bitcast(I32), 0)
-        xs_a = keep.tile([P, 2, 1024], U8, name="xs_a", align_bytes=64)
+        ws0_a = keep.tile([P, SA, 512], U8, name="ws0_a", align_bytes=256)
+        nc.vector.memset(ws0_a[:].bitcast(I32), 0)
+        xs_a = keep.tile([P, SA, 1024], U8, name="xs_a", align_bytes=256)
         nc.vector.memset(xs_a[:].bitcast(I32), 0)
-        xs_b = keep.tile([P, 6, 1024], U8, name="xs_b", align_bytes=64)
+        ws0_b = keep.tile([P, G - SA, 512], U8, name="ws0_b", align_bytes=256)
+        nc.vector.memset(ws0_b[:].bitcast(I32), 0)
+        xs_b = keep.tile([P, G - SA, 1024], U8, name="xs_b", align_bytes=256)
         nc.vector.memset(xs_b[:].bitcast(I32), 0)
 
         chunk_of = []
@@ -70,8 +73,8 @@ def tile_levitattention_pa_kernel(tc, inputs_words, inputs_scales, w_qkv_words, 
         wc0 = []
         xc = []
         for c, (a, b) in enumerate(chunks):
-            wt = keep.tile([P, b - a, 1024], U8, name=f"wc0_{c}", align_bytes=64)
-            xt_ = keep.tile([P, b - a, 2048], U8, name=f"xc_{c}", align_bytes=64)
+            wt = keep.tile([P, b - a, 1024], U8, name=f"wc0_{c}", align_bytes=256)
+            xt_ = keep.tile([P, b - a, 2048], U8, name=f"xc_{c}", align_bytes=256)
             wc0.append(wt)
             xc.append(xt_)
             for g in range(a, b):
@@ -87,13 +90,14 @@ def tile_levitattention_pa_kernel(tc, inputs_words, inputs_scales, w_qkv_words, 
 
         load_w0(0)
         load_x(0)
-        load_scales(ws0, w_qkv_scales[:, :, 512 * first : 512 * first + 512])
-        load_scales(xs_a, inputs_scales[0:2])
+        load_scales(ws0_a, w_qkv_scales[0:SA, :, 512 * first : 512 * first + 512])
+        load_scales(xs_a, inputs_scales[0:SA])
         load_w0(1)
         load_x(1)
-        load_scales(xs_b, inputs_scales[2:8])
         load_w0(2)
         load_x(2)
+        load_scales(ws0_b, w_qkv_scales[SA:G, :, 512 * first : 512 * first + 512])
+        load_scales(xs_b, inputs_scales[SA:G])
         load_w0(3)
         load_x(3)
 
@@ -110,14 +114,14 @@ def tile_levitattention_pa_kernel(tc, inputs_words, inputs_scales, w_qkv_words, 
         nc.gpsimd.dma_start(out=gain_rows[34:36, :], in_=bn_scale[1792:2048].rearrange("(n d) -> n d", n=2))
 
         acc_w = psum.tile([P, PIX], F32, name="acc")
-        for _ in range(7):
+        for _ in range(6):
             nc.tensor.matmul(acc_w[:], warm[:, 0:P], warm[:], start=True, stop=True)
 
         pc0 = []
 
         def permute_w0(c):
             a, b = chunks[c]
-            t = keep.tile([P, b - a, 4, 256], U8, name=f"pc0_{c}", align_bytes=64)
+            t = keep.tile([P, b - a, 4, 256], U8, name=f"pc0_{c}", align_bytes=256)
             for g in range(b - a):
                 nc.vector.tensor_copy(
                     out=t[:, g].rearrange("p i n -> p (i n)").bitcast(I32).rearrange("p (i q w) -> p i q w", i=4, q=4),
@@ -129,31 +133,41 @@ def tile_levitattention_pa_kernel(tc, inputs_words, inputs_scales, w_qkv_words, 
         ring_c = {}
 
         def permute_scales(n, raw, i):
-            t = work.tile([P, G, P], U8, name="perm_s", bufs=6, align_bytes=64)
+            t = work.tile([P, G, P], U8, name="perm_s", bufs=4, align_bytes=256)
             nc.vector.tensor_copy(
                 out=t[:].bitcast(I32).rearrange("p g (q w) -> p g q w", q=4),
                 in_=raw.bitcast(I32).rearrange("p g (q i w) -> p i g q w", q=4, i=4)[:, i],
             )
             ring_s[n] = t
 
+        ps0 = keep.tile([P, G, 4, P], U8, name="ps0", align_bytes=256)
+
+        def permute_s0(raw, a, b):
+            for g in range(a, b):
+                nc.vector.tensor_copy(
+                    out=ps0[:, g].rearrange("p i n -> p (i n)").bitcast(I32).rearrange("p (i q w) -> p i q w", i=4, q=4),
+                    in_=raw[:, g - a].bitcast(I32).rearrange("p (q i w) -> p i q w", q=4, i=4),
+                )
+
         permute_w0(0)
-        for i in range(4):
-            permute_scales(i, ws0[:], i)
+        permute_s0(ws0_a, 0, SA)
         permute_w0(1)
+        permute_w0(2)
+        permute_s0(ws0_b, SA, G)
 
         wg_c = {}
         wg_s = {}
 
         def zero_group(k):
             vs = GROUPS[k]
-            s = keep.tile([P, G, 512 * len(vs)], U8, name=f"wg_s{k}", align_bytes=64)
+            s = keep.tile([P, G, 512 * len(vs)], U8, name=f"wg_s{k}", align_bytes=256)
             nc.vector.memset(s[:].bitcast(I32), 0)
             return s
 
         def load_group(k, s):
             vs = GROUPS[k]
             n = len(vs)
-            c = keep.tile([P, G, 1024 * n], U8, name=f"wg_c{k}", align_bytes=64)
+            c = keep.tile([P, G, 1024 * n], U8, name=f"wg_c{k}", align_bytes=256)
             lo = vs[0]
             load_scales(s, w_qkv_scales[:, :, 512 * lo : 512 * (lo + n)])
             load_codes(c, w_qkv_words[:, :, 1024 * lo : 1024 * (lo + n)])
@@ -161,7 +175,6 @@ def tile_levitattention_pa_kernel(tc, inputs_words, inputs_scales, w_qkv_words, 
                 wc_raw[v] = c[:, :, 1024 * x : 1024 * x + 1024]
                 ws_raw[v] = s[:, :, 512 * x : 512 * x + 512]
 
-        permute_w0(2)
         s1 = zero_group(1)
         load_group(1, s1)
         permute_w0(3)
@@ -170,7 +183,7 @@ def tile_levitattention_pa_kernel(tc, inputs_words, inputs_scales, w_qkv_words, 
             load_group(k, sk)
 
         def permute(n):
-            t = work.tile([P, G, 256], U8, name="perm_c", bufs=4, align_bytes=64)
+            t = work.tile([P, G, 256], U8, name="perm_c", bufs=4, align_bytes=256)
             out = t[:].bitcast(I32).rearrange("p g (q w) -> p g q w", q=4)
             if n < 28:
                 v, i = UNITS[n // 4], n % 4
@@ -180,7 +193,7 @@ def tile_levitattention_pa_kernel(tc, inputs_words, inputs_scales, w_qkv_words, 
                 permute_scales(n, ws_raw[v], i)
             else:
                 i = n - 28
-                s = work.tile([P, G, P], U8, name="perm_s", bufs=6, align_bytes=64)
+                s = work.tile([P, G, P], U8, name="perm_s", bufs=4, align_bytes=256)
                 out_s = s[:].bitcast(I32).rearrange("p g (q w) -> p g q w", q=4)
                 raw_c = wc_raw[SPECIAL][:, :, 0:512].bitcast(I32).rearrange("p g (h s i w) -> p i s g h w", h=2, s=2, i=2)
                 raw_s = ws_raw[SPECIAL][:, :, 0:256].bitcast(I32).rearrange("p g (h s i w) -> p i s g h w", h=2, s=2, i=2)
@@ -198,7 +211,7 @@ def tile_levitattention_pa_kernel(tc, inputs_words, inputs_scales, w_qkv_words, 
             if n < 4:
                 c, k = chunk_of[g]
                 w_c = pc0[c][:, k, n, :]
-                w_s = ring_s[n][:, g, :]
+                w_s = ps0[:, g, n, :]
             elif n < 30:
                 w_c = ring_c[n][:, g, :]
                 w_s = ring_s[n][:, g, :]
@@ -207,7 +220,7 @@ def tile_levitattention_pa_kernel(tc, inputs_words, inputs_scales, w_qkv_words, 
                 w_c = wc_raw[SPECIAL][:, g, 256 * h : 256 * h + 256]
                 w_s = ws_raw[SPECIAL][:, g, 128 * h : 128 * h + 128]
             c, k = chunk_of[g]
-            x_s = xs_a[:, g] if g < 2 else xs_b[:, g - 2]
+            x_s = xs_a[:, g] if g < SA else xs_b[:, g - SA]
             nc.tensor.matmul_mx(
                 out=acc[(n, m)][:, lo:hi],
                 lhsT=w_c.bitcast(FP4),
@@ -234,17 +247,19 @@ def tile_levitattention_pa_kernel(tc, inputs_words, inputs_scales, w_qkv_words, 
             nc.vector.bn_aggr(out=mv[:], in_=stat[n][:, 0:parts, :].rearrange("p a b -> p (a b)"))
             rstd = work.tile([P, 1], F32, name="rstd", bufs=3)
             nc.scalar.activation(out=rstd[:], in_=mv[:, 1:2], func=ACT.Abs_reciprocal_sqrt, bias=EPS, scale=1.0)
-            coef[n] = (mv, rstd)
+            col = 8 * (n % 4) + UNITS[n // 4] if n < 28 else 32 + n - 28
+            minus = work.tile([P, 1], F32, name="minus", bufs=3)
+            nc.vector.scalar_tensor_tensor(
+                out=minus[:], in0=mv[:, 0:1], scalar=-1.0, in1=gain[:, col : col + 1], op0=ALU.mult, op1=ALU.mult
+            )
+            coef[n] = (minus, rstd, gain[:, col : col + 1])
 
         def factors(n):
-            mv, rstd = coef[n]
-            col = 8 * (n % 4) + UNITS[n // 4] if n < 28 else 32 + n - 28
+            minus, rstd, g = coef[n]
             scale = work.tile([P, 1], F32, name="scale", bufs=3)
             shift = work.tile([P, 1], F32, name="shift", bufs=3)
-            nc.vector.tensor_mul(out=scale[:], in0=rstd[:], in1=gain[:, col : col + 1])
-            nc.vector.scalar_tensor_tensor(
-                out=shift[:], in0=mv[:, 0:1], scalar=-1.0, in1=scale[:], op0=ALU.mult, op1=ALU.mult
-            )
+            nc.vector.tensor_mul(out=scale[:], in0=rstd[:], in1=g)
+            nc.vector.tensor_mul(out=shift[:], in0=rstd[:], in1=minus[:])
             coef[n] = (scale, shift)
 
         xn = {}
@@ -256,11 +271,11 @@ def tile_levitattention_pa_kernel(tc, inputs_words, inputs_scales, w_qkv_words, 
                     u = n // 4
                     tiles = 4 if n < 28 else 2
                     if (u, m) not in xn:
-                        xn[(u, m)] = work.tile([P, 16, tiles, 32], F32, name="xn", bufs=4, align_bytes=64)
+                        xn[(u, m)] = work.tile([P, 16, tiles, 32], F32, name="xn", bufs=4, align_bytes=256)
                     dst = xn[(u, m)][:, :, n % 4, :]
                     src = acc[(n, m)][:].rearrange("p (t j) -> p j t", j=16)
                 else:
-                    xn[(n, m)] = work.tile([P, 4, P], F32, name="xnat", bufs=4, align_bytes=64)
+                    xn[(n, m)] = work.tile([P, 4, P], F32, name="xnat", bufs=4, align_bytes=256)
                     dst = xn[(n, m)][:]
                     src = acc[(n, m)][:].rearrange("p (t j) -> p j t", j=4)
                 nc.scalar.activation(out=dst, in_=src, func=ACT.Identity, bias=shift[:], scale=scale[:])
@@ -270,7 +285,7 @@ def tile_levitattention_pa_kernel(tc, inputs_words, inputs_scales, w_qkv_words, 
         def turn(u, m, half):
             tiles = 4 if u < 7 else 2
             if (u, m) not in xt:
-                xt[(u, m)] = work.tile([P, 16, tiles, 32], F32, name="xt", bufs=4, align_bytes=64)
+                xt[(u, m)] = work.tile([P, 16, tiles, 32], F32, name="xt", bufs=4, align_bytes=256)
             lo, hi = (8 * half, 8 * half + 8) if half is not None else (0, 16)
             nc.vector.transpose(
                 out=xt[(u, m)][:, lo:hi].rearrange("p j i c -> p (j i c)"),
@@ -370,42 +385,46 @@ def tile_levitattention_pa_kernel(tc, inputs_words, inputs_scales, w_qkv_words, 
             for j in range(lo, hi):
                 nc.tensor.transpose(bank[:, P * j : P * j + P], xn[(n, m)][:, j, :], ident_f[:])
 
-        res = {}
+        def out_rows(m, h, a, b):
+            return out_1[m, h].rearrange("(t j) d -> t j d", j=4)[:, a:b, :]
+
+        banks = []
         for m in range(MAPS):
             bank = psum.tile([P, PIX], F32, name="acc")
             turn_natural(30, m, 0, 4, bank)
-            res[m] = work.tile([P, 4, P], F32, name="res", bufs=4, align_bytes=64)
-            acc[(30, m)] = bank
-        nc.scalar.copy(out=res[0][:].rearrange("p j d -> p (j d)"), in_=acc[(30, 0)][:])
+            banks.append(bank)
         aggregate(31, parts=3)
-        nc.vector.tensor_copy(out=res[1][:].rearrange("p j d -> p (j d)"), in_=acc[(30, 1)][:])
+        res = []
         for m in range(MAPS):
-            nc.sync.dma_start(out=out_1[m, 6].rearrange("(t j) d -> t j d", j=4), in_=res[m][:])
+            r = work.tile([P, 4, P], F32, name="res", bufs=4, align_bytes=64)
+            res.append(r)
+        nc.scalar.copy(out=res[0][:].rearrange("p j d -> p (j d)"), in_=banks[0][:])
+        nc.vector.tensor_copy(out=res[1][:].rearrange("p j d -> p (j d)"), in_=banks[1][:])
+        for m in range(MAPS):
+            nc.sync.dma_start(out=out_rows(m, 6, 0, 4), in_=res[m][:])
         factors(31)
         scale, shift = coef[31]
-        xl = []
-        banks = []
-        last = []
         for m in range(MAPS):
-            t = work.tile([P, 4, P], F32, name="xnat", bufs=4, align_bytes=64)
-            xl.append(t)
+            t = work.tile([P, 4, P], F32, name="xnat", bufs=4, align_bytes=256)
             xn[(31, m)] = t
-            r = work.tile([P, 4, P], F32, name="res", bufs=4, align_bytes=64)
-            last.append(r)
         for half in range(2):
             a, b = 2 * half, 2 * half + 2
             src = [acc[(31, m)][:].rearrange("p (t j) -> p j t", j=4)[:, a:b, :] for m in range(MAPS)]
-            nc.scalar.activation(out=xl[0][:, a:b, :], in_=src[0], func=ACT.Identity, bias=shift[:], scale=scale[:])
-            nc.vector.tensor_scalar(
-                out=xl[1][:, a:b, :], in0=src[1], scalar1=scale[:], scalar2=shift[:], op0=ALU.mult, op1=ALU.add
+            nc.scalar.activation(
+                out=xn[(31, 0)][:, a:b, :], in_=src[0], func=ACT.Identity, bias=shift[:], scale=scale[:]
             )
-        for m in range(MAPS):
-            bank = psum.tile([P, PIX], F32, name="acc")
-            banks.append(bank)
+            nc.vector.tensor_scalar(
+                out=xn[(31, 1)][:, a:b, :], in0=src[1], scalar1=scale[:], scalar2=shift[:], op0=ALU.mult, op1=ALU.add
+            )
         for half in range(2):
+            a, b = 2 * half, 2 * half + 2
             for m in range(MAPS):
-                turn_natural(31, m, 2 * half, 2 * half + 2, banks[m])
-        nc.scalar.copy(out=last[0][:].rearrange("p j d -> p (j d)"), in_=banks[0][:])
-        nc.vector.tensor_copy(out=last[1][:].rearrange("p j d -> p (j d)"), in_=banks[1][:])
-        nc.scalar.dma_start(out=out_1[0, 7].rearrange("(t j) d -> t j d", j=4), in_=last[0][:])
-        nc.sync.dma_start(out=out_1[1, 7].rearrange("(t j) d -> t j d", j=4), in_=last[1][:])
+                bank = psum.tile([P, 2, P], F32, name="acc")
+                for j in range(2):
+                    nc.tensor.transpose(bank[:, j, :], xn[(31, m)][:, a + j, :], ident_f[:])
+                r = work.tile([P, 2, P], F32, name="last", bufs=4, align_bytes=64)
+                if m == 0:
+                    nc.scalar.copy(out=r[:], in_=bank[:])
+                else:
+                    nc.vector.tensor_copy(out=r[:], in_=bank[:])
+                nc.sync.dma_start(out=out_rows(m, 7, a, b), in_=r[:])

@@ -42,7 +42,7 @@ def tile_levitattention_pa_kernel(tc, inputs_words, inputs_scales, w_qkv_words, 
             return ap.bitcast(I32)
 
         def load_scales(dst, src):
-            for q in range(4):
+            for q in (0, 2, 1, 3):
                 nc.sync.dma_start(
                     out=words(dst[32 * q : 32 * q + 4, :, :]),
                     in_=words(src[:, 4 * q : 4 * q + 4, :].rearrange("g r n -> r g n")),
@@ -134,7 +134,7 @@ def tile_levitattention_pa_kernel(tc, inputs_words, inputs_scales, w_qkv_words, 
 
         def permute_scales(n, raw, i):
             t = work.tile([P, G, P], U8, name="perm_s", bufs=4, align_bytes=256)
-            nc.vector.tensor_copy(
+            nc.gpsimd.tensor_copy(
                 out=t[:].bitcast(I32).rearrange("p g (q w) -> p g q w", q=4),
                 in_=raw.bitcast(I32).rearrange("p g (q i w) -> p i g q w", q=4, i=4)[:, i],
             )
@@ -187,7 +187,7 @@ def tile_levitattention_pa_kernel(tc, inputs_words, inputs_scales, w_qkv_words, 
             out = t[:].bitcast(I32).rearrange("p g (q w) -> p g q w", q=4)
             if n < 28:
                 v, i = UNITS[n // 4], n % 4
-                nc.vector.tensor_copy(
+                nc.gpsimd.tensor_copy(
                     out=out, in_=wc_raw[v].bitcast(I32).rearrange("p g (q i w) -> p i g q w", q=4, i=4)[:, i]
                 )
                 permute_scales(n, ws_raw[v], i)
@@ -198,8 +198,8 @@ def tile_levitattention_pa_kernel(tc, inputs_words, inputs_scales, w_qkv_words, 
                 raw_c = wc_raw[SPECIAL][:, :, 0:512].bitcast(I32).rearrange("p g (h s i w) -> p i s g h w", h=2, s=2, i=2)
                 raw_s = ws_raw[SPECIAL][:, :, 0:256].bitcast(I32).rearrange("p g (h s i w) -> p i s g h w", h=2, s=2, i=2)
                 for half in range(2):
-                    nc.vector.tensor_copy(out=out[:, :, 2 * half : 2 * half + 2], in_=raw_c[:, i, half])
-                    nc.vector.tensor_copy(out=out_s[:, :, 2 * half : 2 * half + 2], in_=raw_s[:, i, half])
+                    nc.gpsimd.tensor_copy(out=out[:, :, 2 * half : 2 * half + 2], in_=raw_c[:, i, half])
+                    nc.gpsimd.tensor_copy(out=out_s[:, :, 2 * half : 2 * half + 2], in_=raw_s[:, i, half])
                 ring_s[n] = s
             ring_c[n] = t
 
@@ -249,8 +249,8 @@ def tile_levitattention_pa_kernel(tc, inputs_words, inputs_scales, w_qkv_words, 
             nc.scalar.activation(out=rstd[:], in_=mv[:, 1:2], func=ACT.Abs_reciprocal_sqrt, bias=EPS, scale=1.0)
             col = 8 * (n % 4) + UNITS[n // 4] if n < 28 else 32 + n - 28
             minus = work.tile([P, 1], F32, name="minus", bufs=3)
-            nc.vector.scalar_tensor_tensor(
-                out=minus[:], in0=mv[:, 0:1], scalar=-1.0, in1=gain[:, col : col + 1], op0=ALU.mult, op1=ALU.mult
+            nc.vector.tensor_scalar(
+                out=minus[:], in0=mv[:, 0:1], scalar1=gain[:, col : col + 1], scalar2=-1.0, op0=ALU.mult, op1=ALU.mult
             )
             coef[n] = (minus, rstd, gain[:, col : col + 1])
 
@@ -258,8 +258,8 @@ def tile_levitattention_pa_kernel(tc, inputs_words, inputs_scales, w_qkv_words, 
             minus, rstd, g = coef[n]
             scale = work.tile([P, 1], F32, name="scale", bufs=3)
             shift = work.tile([P, 1], F32, name="shift", bufs=3)
-            nc.vector.tensor_mul(out=scale[:], in0=rstd[:], in1=g)
-            nc.vector.tensor_mul(out=shift[:], in0=rstd[:], in1=minus[:])
+            nc.scalar.activation(out=scale[:], in_=rstd[:], func=ACT.Copy, scale=g)
+            nc.scalar.activation(out=shift[:], in_=rstd[:], func=ACT.Copy, scale=minus[:])
             coef[n] = (scale, shift)
 
         xn = {}

@@ -51,6 +51,10 @@ def tile_levitattention_pa_kernel(tc, inputs_words, inputs_scales, w_qkv_words, 
         def load_codes(dst, src):
             nc.sync.dma_start(out=words(dst[:, :, :]), in_=words(src.rearrange("g p n -> p g n")))
 
+        def shifted(pool, width, start, name, bufs):
+            t = pool.tile([P, width + start], U8, name=name, bufs=bufs, align_bytes=256)
+            return t[:, start : start + width]
+
         warm = keep.tile([P, PIX], BF16, name="warm")
         nc.gpsimd.memset(warm[:], 0.0)
         gain_rows = keep.tile([P, P], BF16, name="gain_rows")
@@ -61,12 +65,12 @@ def tile_levitattention_pa_kernel(tc, inputs_words, inputs_scales, w_qkv_words, 
         wc_raw = {}
         ws0_a = keep.tile([P, SA, 512], U8, name="ws0_a", align_bytes=256)
         nc.vector.memset(ws0_a[:].bitcast(I32), 0)
-        xs_a = keep.tile([P, SA, 1024], U8, name="xs_a", align_bytes=256)
-        nc.vector.memset(xs_a[:].bitcast(I32), 0)
+        xs_a = shifted(keep, SA * 1024, 192, "xs_a", 1).rearrange("p (g n) -> p g n", g=SA)
+        nc.vector.memset(xs_a.bitcast(I32), 0)
         ws0_b = keep.tile([P, G - SA, 512], U8, name="ws0_b", align_bytes=256)
         nc.vector.memset(ws0_b[:].bitcast(I32), 0)
-        xs_b = keep.tile([P, G - SA, 1024], U8, name="xs_b", align_bytes=256)
-        nc.vector.memset(xs_b[:].bitcast(I32), 0)
+        xs_b = shifted(keep, (G - SA) * 1024, 192, "xs_b", 1).rearrange("p (g n) -> p g n", g=G - SA)
+        nc.vector.memset(xs_b.bitcast(I32), 0)
 
         chunk_of = []
         chunks = [(0, 1), (1, 2), (2, 4), (4, 8)]
@@ -114,6 +118,7 @@ def tile_levitattention_pa_kernel(tc, inputs_words, inputs_scales, w_qkv_words, 
         nc.gpsimd.dma_start(out=gain_rows[34:36, :], in_=bn_scale[1792:2048].rearrange("(n d) -> n d", n=2))
 
         acc_w = psum.tile([P, PIX], F32, name="acc")
+        gain_p = psum.tile([P, P], BF16, name="acc")
         for _ in range(6):
             nc.tensor.matmul(acc_w[:], warm[:, 0:P], warm[:], start=True, stop=True)
 
@@ -133,9 +138,9 @@ def tile_levitattention_pa_kernel(tc, inputs_words, inputs_scales, w_qkv_words, 
         ring_c = {}
 
         def permute_scales(n, raw, i):
-            t = work.tile([P, G, P], U8, name="perm_s", bufs=4, align_bytes=256)
+            t = shifted(work, G * P, 64, "perm_s", 4).rearrange("p (g n) -> p g n", g=G)
             nc.gpsimd.tensor_copy(
-                out=t[:].bitcast(I32).rearrange("p g (q w) -> p g q w", q=4),
+                out=t.bitcast(I32).rearrange("p g (q w) -> p g q w", q=4),
                 in_=raw.bitcast(I32).rearrange("p g (q i w) -> p i g q w", q=4, i=4)[:, i],
             )
             ring_s[n] = t
@@ -183,8 +188,8 @@ def tile_levitattention_pa_kernel(tc, inputs_words, inputs_scales, w_qkv_words, 
             load_group(k, sk)
 
         def permute(n):
-            t = work.tile([P, G, 256], U8, name="perm_c", bufs=4, align_bytes=256)
-            out = t[:].bitcast(I32).rearrange("p g (q w) -> p g q w", q=4)
+            t = shifted(work, G * 256, 128, "perm_c", 4).rearrange("p (g n) -> p g n", g=G)
+            out = t.bitcast(I32).rearrange("p g (q w) -> p g q w", q=4)
             if n < 28:
                 v, i = UNITS[n // 4], n % 4
                 nc.gpsimd.tensor_copy(
@@ -193,8 +198,8 @@ def tile_levitattention_pa_kernel(tc, inputs_words, inputs_scales, w_qkv_words, 
                 permute_scales(n, ws_raw[v], i)
             else:
                 i = n - 28
-                s = work.tile([P, G, P], U8, name="perm_s", bufs=4, align_bytes=256)
-                out_s = s[:].bitcast(I32).rearrange("p g (q w) -> p g q w", q=4)
+                s = shifted(work, G * P, 64, "perm_s", 4).rearrange("p (g n) -> p g n", g=G)
+                out_s = s.bitcast(I32).rearrange("p g (q w) -> p g q w", q=4)
                 raw_c = wc_raw[SPECIAL][:, :, 0:512].bitcast(I32).rearrange("p g (h s i w) -> p i s g h w", h=2, s=2, i=2)
                 raw_s = ws_raw[SPECIAL][:, :, 0:256].bitcast(I32).rearrange("p g (h s i w) -> p i s g h w", h=2, s=2, i=2)
                 for half in range(2):
@@ -206,8 +211,8 @@ def tile_levitattention_pa_kernel(tc, inputs_words, inputs_scales, w_qkv_words, 
         acc = {}
 
         def one_pass(n, m, g, lo=0, hi=PIX):
-            if (n, m) not in acc:
-                acc[(n, m)] = psum.tile([P, PIX], F32, name="acc")
+            if (n, m, lo) not in acc:
+                acc[(n, m, lo)] = psum.tile([P, hi - lo], F32, name="acc")
             if n < 4:
                 c, k = chunk_of[g]
                 w_c = pc0[c][:, k, n, :]
@@ -222,7 +227,7 @@ def tile_levitattention_pa_kernel(tc, inputs_words, inputs_scales, w_qkv_words, 
             c, k = chunk_of[g]
             x_s = xs_a[:, g] if g < SA else xs_b[:, g - SA]
             nc.tensor.matmul_mx(
-                out=acc[(n, m)][:, lo:hi],
+                out=acc[(n, m, lo)][:],
                 lhsT=w_c.bitcast(FP4),
                 lhsT_scale=w_s,
                 rhs=xc[c][:, k, 1024 * m + 2 * lo : 1024 * m + 2 * hi].bitcast(FP4),
@@ -233,11 +238,11 @@ def tile_levitattention_pa_kernel(tc, inputs_words, inputs_scales, w_qkv_words, 
 
         stat = {}
 
-        def stats(n, m, lo=0, hi=PIX, slot=None):
+        def stats(n, m, lo=0, slot=None):
             if n not in stat:
                 stat[n] = work.tile([P, 3, 6], F32, name="stat", bufs=3)
             k = m if slot is None else slot
-            nc.vector.bn_stats(out=stat[n][:, k, :], in_=acc[(n, m)][:, lo:hi])
+            nc.vector.bn_stats(out=stat[n][:, k, :], in_=acc[(n, m, lo)][:])
 
         gain = keep.tile([P, 36], F32, name="gain")
         coef = {}
@@ -258,34 +263,38 @@ def tile_levitattention_pa_kernel(tc, inputs_words, inputs_scales, w_qkv_words, 
             minus, rstd, g = coef[n]
             scale = work.tile([P, 1], F32, name="scale", bufs=3)
             shift = work.tile([P, 1], F32, name="shift", bufs=3)
-            nc.scalar.activation(out=scale[:], in_=rstd[:], func=ACT.Copy, scale=g)
-            nc.scalar.activation(out=shift[:], in_=rstd[:], func=ACT.Copy, scale=minus[:])
+            if n < 31:
+                nc.scalar.activation(out=scale[:], in_=rstd[:], func=ACT.Copy, scale=g)
+                nc.scalar.activation(out=shift[:], in_=rstd[:], func=ACT.Copy, scale=minus[:])
+            else:
+                nc.vector.tensor_mul(out=scale[:], in0=rstd[:], in1=g)
+                nc.vector.tensor_mul(out=shift[:], in0=rstd[:], in1=minus[:])
             coef[n] = (scale, shift)
 
         xn = {}
 
+        def width(u):
+            return 4 if u < 7 else 9 - u
+
         def normalise(n):
             scale, shift = coef[n]
             for m in range(MAPS):
-                if n < 30:
-                    u = n // 4
-                    tiles = 4 if n < 28 else 2
+                if n < 31:
+                    u = min(n // 4, 7) if n < 30 else 8
+                    tiles = width(u)
                     if (u, m) not in xn:
                         xn[(u, m)] = work.tile([P, 16, tiles, 32], F32, name="xn", bufs=4, align_bytes=256)
-                    dst = xn[(u, m)][:, :, n % 4, :]
-                    src = acc[(n, m)][:].rearrange("p (t j) -> p j t", j=16)
-                else:
-                    xn[(n, m)] = work.tile([P, 4, P], F32, name="xnat", bufs=4, align_bytes=256)
-                    dst = xn[(n, m)][:]
-                    src = acc[(n, m)][:].rearrange("p (t j) -> p j t", j=4)
+                    dst = xn[(u, m)][:, :, n % 4 if n < 30 else 0, :]
+                    src = acc[(n, m, 0)][:].rearrange("p (t j) -> p j t", j=16)
                 nc.scalar.activation(out=dst, in_=src, func=ACT.Identity, bias=shift[:], scale=scale[:])
 
         xt = {}
 
         def turn(u, m, half):
-            tiles = 4 if u < 7 else 2
+            tiles = width(u)
             if (u, m) not in xt:
-                xt[(u, m)] = work.tile([P, 16, tiles, 32], F32, name="xt", bufs=4, align_bytes=256)
+                tag = "xt" if u < 7 else f"xt_{u}"
+                xt[(u, m)] = work.tile([P, 16, tiles, 32], F32, name=tag, bufs=3 if u < 7 else 2, align_bytes=256)
             lo, hi = (8 * half, 8 * half + 8) if half is not None else (0, 16)
             nc.vector.transpose(
                 out=xt[(u, m)][:, lo:hi].rearrange("p j i c -> p (j i c)"),
@@ -304,6 +313,12 @@ def tile_levitattention_pa_kernel(tc, inputs_words, inputs_scales, w_qkv_words, 
                 else:
                     dst = out_2[m, h0 : h0 + 4, :, P * (quarter - 2) : P * (quarter - 1)]
                 nc.sync.dma_start(out=dst.rearrange("h (t j) d -> (h t) j d", j=16), in_=src)
+            elif u == 8:
+                for q in range(4):
+                    nc.sync.dma_start(
+                        out=out_1[m, 6, :, 32 * q : 32 * q + 32].rearrange("(t j) d -> t j d", j=16),
+                        in_=src[32 * q : 32 * q + 32],
+                    )
             else:
                 for s in range(2):
                     nc.sync.dma_start(
@@ -316,7 +331,6 @@ def tile_levitattention_pa_kernel(tc, inputs_words, inputs_scales, w_qkv_words, 
                 for n in range(3):
                     one_pass(n, m, g)
 
-        gain_p = psum.tile([P, P], BF16, name="acc")
         nc.tensor.transpose(gain_p[:], gain_rows[:], ident_b[:])
         nc.vector.tensor_copy(out=gain[:], in_=gain_p[:, 0:36])
 
@@ -362,6 +376,8 @@ def tile_levitattention_pa_kernel(tc, inputs_words, inputs_scales, w_qkv_words, 
             for g in range(G):
                 one_pass(n, 0, g)
             stats(n, 0)
+            if n == 28:
+                next_piece()
             for g in range(G):
                 one_pass(n, 1, g)
             if n == 30:
@@ -375,56 +391,39 @@ def tile_levitattention_pa_kernel(tc, inputs_words, inputs_scales, w_qkv_words, 
         for g in range(G):
             one_pass(31, 0, g)
         stats(31, 0)
+        for m in range(MAPS):
+            turn(8, m, None)
+            store(8, m)
         for part in range(2):
             lo = 256 * part
             for g in range(G):
                 one_pass(31, 1, g, lo, lo + 256)
-            stats(31, 1, lo, lo + 256, slot=1 + part)
+            stats(31, 1, lo, slot=1 + part)
 
-        def turn_natural(n, m, lo, hi, bank):
-            for j in range(lo, hi):
-                nc.tensor.transpose(bank[:, P * j : P * j + P], xn[(n, m)][:, j, :], ident_f[:])
-
-        def out_rows(m, h, a, b):
-            return out_1[m, h].rearrange("(t j) d -> t j d", j=4)[:, a:b, :]
-
-        banks = []
-        for m in range(MAPS):
-            bank = psum.tile([P, PIX], F32, name="acc")
-            turn_natural(30, m, 0, 4, bank)
-            banks.append(bank)
         aggregate(31, parts=3)
-        res = []
-        for m in range(MAPS):
-            r = work.tile([P, 4, P], F32, name="res", bufs=4, align_bytes=64)
-            res.append(r)
-        nc.scalar.copy(out=res[0][:].rearrange("p j d -> p (j d)"), in_=banks[0][:])
-        nc.vector.tensor_copy(out=res[1][:].rearrange("p j d -> p (j d)"), in_=banks[1][:])
-        for m in range(MAPS):
-            nc.sync.dma_start(out=out_rows(m, 6, 0, 4), in_=res[m][:])
         factors(31)
         scale, shift = coef[31]
+        flat = []
         for m in range(MAPS):
-            t = work.tile([P, 4, P], F32, name="xnat", bufs=4, align_bytes=256)
-            xn[(31, m)] = t
+            t = work.tile([P, 2, 2, P], F32, name="flat", bufs=2, align_bytes=64)
+            flat.append(t)
         for half in range(2):
-            a, b = 2 * half, 2 * half + 2
-            src = [acc[(31, m)][:].rearrange("p (t j) -> p j t", j=4)[:, a:b, :] for m in range(MAPS)]
-            nc.scalar.activation(
-                out=xn[(31, 0)][:, a:b, :], in_=src[0], func=ACT.Identity, bias=shift[:], scale=scale[:]
-            )
+            src = [acc[(31, 0, 0)][:, 256 * half : 256 * half + 256], acc[(31, 1, 256 * half)][:]]
+            src = [s.rearrange("p (t j) -> p j t", j=2) for s in src]
+            nc.scalar.activation(out=flat[0][:, half], in_=src[0], func=ACT.Identity, bias=shift[:], scale=scale[:])
             nc.vector.tensor_scalar(
-                out=xn[(31, 1)][:, a:b, :], in0=src[1], scalar1=scale[:], scalar2=shift[:], op0=ALU.mult, op1=ALU.add
+                out=flat[1][:, half], in0=src[1], scalar1=scale[:], scalar2=shift[:], op0=ALU.mult, op1=ALU.add
             )
         for half in range(2):
-            a, b = 2 * half, 2 * half + 2
-            for m in range(MAPS):
+            for m in (1, 0):
                 bank = psum.tile([P, 2, P], F32, name="acc")
                 for j in range(2):
-                    nc.tensor.transpose(bank[:, j, :], xn[(31, m)][:, a + j, :], ident_f[:])
+                    nc.tensor.transpose(bank[:, j, :], flat[m][:, half, j, :], ident_f[:])
                 r = work.tile([P, 2, P], F32, name="last", bufs=4, align_bytes=64)
                 if m == 0:
                     nc.scalar.copy(out=r[:], in_=bank[:])
                 else:
                     nc.vector.tensor_copy(out=r[:], in_=bank[:])
-                nc.sync.dma_start(out=out_rows(m, 7, a, b), in_=r[:])
+                nc.sync.dma_start(
+                    out=out_1[m, 7, 256 * half : 256 * half + 256].rearrange("(t j) d -> t j d", j=2), in_=r[:]
+                )

from contextlib import ExitStack

import concourse.mybir as mybir
from concourse.masks import make_identity

F32 = mybir.dt.float32
BF16 = mybir.dt.bfloat16
U8 = mybir.dt.uint8
I32 = mybir.dt.int32
FP4 = mybir.dt.float4_e2m1fn_x4
ACT = mybir.ActivationFunctionType
ALU = mybir.AluOpType

P = 128
G = 8
MAPS = 2
PIX = 512
EPS = 1e-5
SA = 3
FLOPS = 2 * 1024 * 4096 * 4096

UNITS = [4, 5, 6, 7, 0, 1, 2]
SPECIAL = 3
GROUPS = [[4], [5], [6, 7], [0, 1], [2, 3]]


def tile_levitattention_pa_kernel(tc, inputs_words, inputs_scales, w_qkv_words, w_qkv_scales, bn_scale, out_0, out_1, out_2):
    nc = tc.nc
    with ExitStack() as ctx:
        keep = ctx.enter_context(tc.tile_pool(name="keep", bufs=1))
        work = ctx.enter_context(tc.tile_pool(name="work", bufs=1))
        psum = ctx.enter_context(tc.psum_pool(name="psum", bufs=8))

        ident_f = keep.tile([P, P], F32, name="ident_f")
        make_identity(nc, ident_f[:])
        ident_b = keep.tile([P, P], BF16, name="ident_b")
        make_identity(nc, ident_b[:])

        ctx.enter_context(tc.manual_schedule())

        def words(ap):
            return ap.bitcast(I32)

        def load_scales(dst, src):
            for q in (0, 2, 1, 3):
                nc.sync.dma_start(
                    out=words(dst[32 * q : 32 * q + 4, :, :]),
                    in_=words(src[:, 4 * q : 4 * q + 4, :].rearrange("g r n -> r g n")),
                )

        def load_codes(dst, src):
            nc.sync.dma_start(out=words(dst[:, :, :]), in_=words(src.rearrange("g p n -> p g n")))

        def shifted(pool, width, start, name, bufs):
            t = pool.tile([P, width + start], U8, name=name, bufs=bufs, align_bytes=256)
            return t[:, start : start + width]

        warm = keep.tile([P, PIX], BF16, name="warm")
        nc.gpsimd.memset(warm[:], 0.0)
        gain_rows = keep.tile([P, P], BF16, name="gain_rows")
        nc.gpsimd.memset(gain_rows[:], 0.0)

        first = UNITS[0]
        ws_raw = {}
        wc_raw = {}
        ws0_a = keep.tile([P, SA, 512], U8, name="ws0_a", align_bytes=256)
        nc.vector.memset(ws0_a[:].bitcast(I32), 0)
        xs_a = shifted(keep, SA * 1024, 192, "xs_a", 1).rearrange("p (g n) -> p g n", g=SA)
        nc.vector.memset(xs_a.bitcast(I32), 0)
        ws0_b = keep.tile([P, G - SA, 512], U8, name="ws0_b", align_bytes=256)
        nc.vector.memset(ws0_b[:].bitcast(I32), 0)
        xs_b = shifted(keep, (G - SA) * 1024, 192, "xs_b", 1).rearrange("p (g n) -> p g n", g=G - SA)
        nc.vector.memset(xs_b.bitcast(I32), 0)

        chunk_of = []
        chunks = [(0, 1), (1, 2), (2, 4), (4, 8)]
        wc0 = []
        xc = []
        for c, (a, b) in enumerate(chunks):
            wt = keep.tile([P, b - a, 1024], U8, name=f"wc0_{c}", align_bytes=256)
            xt_ = keep.tile([P, b - a, 2048], U8, name=f"xc_{c}", align_bytes=256)
            wc0.append(wt)
            xc.append(xt_)
            for g in range(a, b):
                chunk_of.append((c, g - a))

        def load_w0(c):
            a, b = chunks[c]
            load_codes(wc0[c], w_qkv_words[a:b, :, 1024 * first : 1024 * first + 1024])

        def load_x(c):
            a, b = chunks[c]
            load_codes(xc[c], inputs_words[a:b, :, :])

        load_w0(0)
        load_x(0)
        load_scales(ws0_a, w_qkv_scales[0:SA, :, 512 * first : 512 * first + 512])
        load_scales(xs_a, inputs_scales[0:SA])
        load_w0(1)
        load_x(1)
        load_w0(2)
        load_x(2)
        load_scales(ws0_b, w_qkv_scales[SA:G, :, 512 * first : 512 * first + 512])
        load_scales(xs_b, inputs_scales[SA:G])
        load_w0(3)
        load_x(3)

        by_tile = bn_scale.rearrange("(v q i c) -> i v q c", v=8, q=4, i=4)
        for i in range(4):
            nc.gpsimd.dma_start(
                out=gain_rows[8 * i : 8 * i + 8, :].rearrange("v (q c) -> v q c", q=4), in_=by_tile[i]
            )
        pair = bn_scale[1536:1792].rearrange("(one h s i c) -> i one s h c", one=1, h=2, s=2, i=2)
        for i in range(2):
            nc.gpsimd.dma_start(
                out=gain_rows[32 + i : 33 + i, :].rearrange("v (s h c) -> v s h c", s=2, h=2), in_=pair[i]
            )
        nc.gpsimd.dma_start(out=gain_rows[34:36, :], in_=bn_scale[1792:2048].rearrange("(n d) -> n d", n=2))

        acc_w = psum.tile([P, PIX], F32, name="acc")
        gain_p = psum.tile([P, P], BF16, name="acc")
        for _ in range(6):
            nc.tensor.matmul(acc_w[:], warm[:, 0:P], warm[:], start=True, stop=True)

        pc0 = []

        def permute_w0(c):
            a, b = chunks[c]
            t = keep.tile([P, b - a, 4, 256], U8, name=f"pc0_{c}", align_bytes=256)
            for g in range(b - a):
                nc.vector.tensor_copy(
                    out=t[:, g].rearrange("p i n -> p (i n)").bitcast(I32).rearrange("p (i q w) -> p i q w", i=4, q=4),
                    in_=wc0[c][:, g].bitcast(I32).rearrange("p (q i w) -> p i q w", q=4, i=4),
                )
            pc0.append(t)

        ring_s = {}
        ring_c = {}

        def permute_scales(n, raw, i):
            t = shifted(work, G * P, 64, "perm_s", 4).rearrange("p (g n) -> p g n", g=G)
            nc.gpsimd.tensor_copy(
                out=t.bitcast(I32).rearrange("p g (q w) -> p g q w", q=4),
                in_=raw.bitcast(I32).rearrange("p g (q i w) -> p i g q w", q=4, i=4)[:, i],
            )
            ring_s[n] = t

        ps0 = keep.tile([P, G, 4, P], U8, name="ps0", align_bytes=256)

        def permute_s0(raw, a, b):
            for g in range(a, b):
                nc.vector.tensor_copy(
                    out=ps0[:, g].rearrange("p i n -> p (i n)").bitcast(I32).rearrange("p (i q w) -> p i q w", i=4, q=4),
                    in_=raw[:, g - a].bitcast(I32).rearrange("p (q i w) -> p i q w", q=4, i=4),
                )

        permute_w0(0)
        permute_s0(ws0_a, 0, SA)
        permute_w0(1)
        permute_w0(2)
        permute_s0(ws0_b, SA, G)

        wg_c = {}
        wg_s = {}

        def zero_group(k):
            vs = GROUPS[k]
            s = keep.tile([P, G, 512 * len(vs)], U8, name=f"wg_s{k}", align_bytes=256)
            nc.vector.memset(s[:].bitcast(I32), 0)
            return s

        def load_group(k, s):
            vs = GROUPS[k]
            n = len(vs)
            c = keep.tile([P, G, 1024 * n], U8, name=f"wg_c{k}", align_bytes=256)
            lo = vs[0]
            load_scales(s, w_qkv_scales[:, :, 512 * lo : 512 * (lo + n)])
            load_codes(c, w_qkv_words[:, :, 1024 * lo : 1024 * (lo + n)])
            for x, v in enumerate(vs):
                wc_raw[v] = c[:, :, 1024 * x : 1024 * x + 1024]
                ws_raw[v] = s[:, :, 512 * x : 512 * x + 512]

        s1 = zero_group(1)
        load_group(1, s1)
        permute_w0(3)
        for k in (2, 3, 4):
            sk = zero_group(k)
            load_group(k, sk)

        def permute(n):
            t = shifted(work, G * 256, 128, "perm_c", 4).rearrange("p (g n) -> p g n", g=G)
            out = t.bitcast(I32).rearrange("p g (q w) -> p g q w", q=4)
            if n < 28:
                v, i = UNITS[n // 4], n % 4
                nc.gpsimd.tensor_copy(
                    out=out, in_=wc_raw[v].bitcast(I32).rearrange("p g (q i w) -> p i g q w", q=4, i=4)[:, i]
                )
                permute_scales(n, ws_raw[v], i)
            else:
                i = n - 28
                s = shifted(work, G * P, 64, "perm_s", 4).rearrange("p (g n) -> p g n", g=G)
                out_s = s.bitcast(I32).rearrange("p g (q w) -> p g q w", q=4)
                raw_c = wc_raw[SPECIAL][:, :, 0:512].bitcast(I32).rearrange("p g (h s i w) -> p i s g h w", h=2, s=2, i=2)
                raw_s = ws_raw[SPECIAL][:, :, 0:256].bitcast(I32).rearrange("p g (h s i w) -> p i s g h w", h=2, s=2, i=2)
                for half in range(2):
                    nc.gpsimd.tensor_copy(out=out[:, :, 2 * half : 2 * half + 2], in_=raw_c[:, i, half])
                    nc.gpsimd.tensor_copy(out=out_s[:, :, 2 * half : 2 * half + 2], in_=raw_s[:, i, half])
                ring_s[n] = s
            ring_c[n] = t

        acc = {}

        def one_pass(n, m, g, lo=0, hi=PIX):
            if (n, m, lo) not in acc:
                acc[(n, m, lo)] = psum.tile([P, hi - lo], F32, name="acc")
            if n < 4:
                c, k = chunk_of[g]
                w_c = pc0[c][:, k, n, :]
                w_s = ps0[:, g, n, :]
            elif n < 30:
                w_c = ring_c[n][:, g, :]
                w_s = ring_s[n][:, g, :]
            else:
                h = n - 28
                w_c = wc_raw[SPECIAL][:, g, 256 * h : 256 * h + 256]
                w_s = ws_raw[SPECIAL][:, g, 128 * h : 128 * h + 128]
            c, k = chunk_of[g]
            x_s = xs_a[:, g] if g < SA else xs_b[:, g - SA]
            nc.tensor.matmul_mx(
                out=acc[(n, m, lo)][:],
                lhsT=w_c.bitcast(FP4),
                lhsT_scale=w_s,
                rhs=xc[c][:, k, 1024 * m + 2 * lo : 1024 * m + 2 * hi].bitcast(FP4),
                rhs_scale=x_s[:, PIX * m + lo : PIX * m + hi],
                start=(g == 0),
                stop=(g == G - 1),
            )

        stat = {}

        def stats(n, m, lo=0, slot=None):
            if n not in stat:
                stat[n] = work.tile([P, 3, 6], F32, name="stat", bufs=3)
            k = m if slot is None else slot
            nc.vector.bn_stats(out=stat[n][:, k, :], in_=acc[(n, m, lo)][:])

        gain = keep.tile([P, 36], F32, name="gain")
        coef = {}

        def aggregate(n, parts=2):
            mv = work.tile([P, 2], F32, name="mv", bufs=3)
            nc.vector.bn_aggr(out=mv[:], in_=stat[n][:, 0:parts, :].rearrange("p a b -> p (a b)"))
            rstd = work.tile([P, 1], F32, name="rstd", bufs=3)
            nc.scalar.activation(out=rstd[:], in_=mv[:, 1:2], func=ACT.Abs_reciprocal_sqrt, bias=EPS, scale=1.0)
            col = 8 * (n % 4) + UNITS[n // 4] if n < 28 else 32 + n - 28
            minus = work.tile([P, 1], F32, name="minus", bufs=3)
            nc.vector.tensor_scalar(
                out=minus[:], in0=mv[:, 0:1], scalar1=gain[:, col : col + 1], scalar2=-1.0, op0=ALU.mult, op1=ALU.mult
            )
            coef[n] = (minus, rstd, gain[:, col : col + 1])

        def factors(n):
            minus, rstd, g = coef[n]
            scale = work.tile([P, 1], F32, name="scale", bufs=3)
            shift = work.tile([P, 1], F32, name="shift", bufs=3)
            if n < 31:
                nc.scalar.activation(out=scale[:], in_=rstd[:], func=ACT.Copy, scale=g)
                nc.scalar.activation(out=shift[:], in_=rstd[:], func=ACT.Copy, scale=minus[:])
            else:
                nc.vector.tensor_mul(out=scale[:], in0=rstd[:], in1=g)
                nc.vector.tensor_mul(out=shift[:], in0=rstd[:], in1=minus[:])
            coef[n] = (scale, shift)

        xn = {}

        def width(u):
            return 4 if u < 7 else 9 - u

        def normalise(n):
            scale, shift = coef[n]
            for m in range(MAPS):
                if n < 31:
                    u = min(n // 4, 7) if n < 30 else 8
                    tiles = width(u)
                    if (u, m) not in xn:
                        xn[(u, m)] = work.tile([P, 16, tiles, 32], F32, name="xn", bufs=4, align_bytes=256)
                    dst = xn[(u, m)][:, :, n % 4 if n < 30 else 0, :]
                    src = acc[(n, m, 0)][:].rearrange("p (t j) -> p j t", j=16)
                nc.scalar.activation(out=dst, in_=src, func=ACT.Identity, bias=shift[:], scale=scale[:])

        xt = {}

        def turn(u, m, half):
            tiles = width(u)
            if (u, m) not in xt:
                tag = "xt" if u < 7 else f"xt_{u}"
                xt[(u, m)] = work.tile([P, 16, tiles, 32], F32, name=tag, bufs=3 if u < 7 else 2, align_bytes=256)
            lo, hi = (8 * half, 8 * half + 8) if half is not None else (0, 16)
            nc.vector.transpose(
                out=xt[(u, m)][:, lo:hi].rearrange("p j i c -> p (j i c)"),
                in_=xn[(u, m)][:, lo:hi].rearrange("p j i t -> p (j i t)"),
            )

        def store(u, m):
            src = xt[(u, m)][:].rearrange("p j i c -> p j (i c)")
            if u < 7:
                v = UNITS[u]
                quarter, h0 = v // 2, 4 * (v % 2)
                if quarter == 0:
                    dst = out_0[m, h0 : h0 + 4]
                elif quarter == 1:
                    dst = out_1[m, h0 : h0 + 4]
                else:
                    dst = out_2[m, h0 : h0 + 4, :, P * (quarter - 2) : P * (quarter - 1)]
                nc.sync.dma_start(out=dst.rearrange("h (t j) d -> (h t) j d", j=16), in_=src)
            elif u == 8:
                for q in range(4):
                    nc.sync.dma_start(
                        out=out_1[m, 6, :, 32 * q : 32 * q + 32].rearrange("(t j) d -> t j d", j=16),
                        in_=src[32 * q : 32 * q + 32],
                    )
            else:
                for s in range(2):
                    nc.sync.dma_start(
                        out=out_1[m, 4:6, :, 64 * s : 64 * s + 64].rearrange("h (t j) d -> (h t) j d", j=16),
                        in_=src[64 * s : 64 * s + 64],
                    )

        for g in range(G):
            for m in range(MAPS):
                for n in range(3):
                    one_pass(n, m, g)

        nc.tensor.transpose(gain_p[:], gain_rows[:], ident_b[:])
        nc.vector.tensor_copy(out=gain[:], in_=gain_p[:, 0:36])

        pieces = []

        def finish(n, between=None):
            aggregate(n)
            if between is not None:
                permute(between)
            factors(n)
            normalise(n)
            if n % 4 == 3 and n < 28:
                for m in range(MAPS):
                    for half in range(2):
                        pieces.append((n // 4, m, half))

        def next_piece():
            if pieces:
                u, m, half = pieces.pop(0)
                turn(u, m, half)
                if half == 1:
                    store(u, m)

        for g in range(G):
            one_pass(3, 0, g)
        for g in range(G):
            one_pass(3, 1, g)
        for n in range(3):
            stats(n, 0)
            stats(n, 1)
            finish(n, between=4 + n if n < 2 else None)
        stats(3, 0)

        for n in range(4, 31):
            stats(n - 1, 1)
            if n - 1 >= 4 or n == 4:
                ready = 0 if n == 4 else len(pieces)
            finish(n - 1, between=n + 2 if n + 2 < 30 else None)
            if ready:
                next_piece()
                if n >= 29:
                    next_piece()
            for g in range(G):
                one_pass(n, 0, g)
            stats(n, 0)
            if n == 28:
                next_piece()
            for g in range(G):
                one_pass(n, 1, g)
            if n == 30:
                turn(7, 0, None)
                store(7, 0)

        stats(30, 1)
        finish(30)
        turn(7, 1, None)
        store(7, 1)
        for g in range(G):
            one_pass(31, 0, g)
        stats(31, 0)
        for m in range(MAPS):
            turn(8, m, None)
            store(8, m)
        for part in range(2):
            lo = 256 * part
            for g in range(G):
                one_pass(31, 1, g, lo, lo + 256)
            stats(31, 1, lo, slot=1 + part)

        aggregate(31, parts=3)
        factors(31)
        scale, shift = coef[31]
        flat = []
        for m in range(MAPS):
            t = work.tile([P, 2, 2, P], F32, name="flat", bufs=2, align_bytes=64)
            flat.append(t)
        for half in range(2):
            src = [acc[(31, 0, 0)][:, 256 * half : 256 * half + 256], acc[(31, 1, 256 * half)][:]]
            src = [s.rearrange("p (t j) -> p j t", j=2) for s in src]
            nc.scalar.activation(out=flat[0][:, half], in_=src[0], func=ACT.Identity, bias=shift[:], scale=scale[:])
            nc.vector.tensor_scalar(
                out=flat[1][:, half], in0=src[1], scalar1=scale[:], scalar2=shift[:], op0=ALU.mult, op1=ALU.add
            )
        for half in range(2):
            for m in (1, 0):
                bank = psum.tile([P, 2, P], F32, name="acc")
                for j in range(2):
                    nc.tensor.transpose(bank[:, j, :], flat[m][:, half, j, :], ident_f[:])
                r = work.tile([P, 2, P], F32, name="last", bufs=4, align_bytes=64)
                if m == 0:
                    nc.scalar.copy(out=r[:], in_=bank[:])
                else:
                    nc.vector.tensor_copy(out=r[:], in_=bank[:])
                nc.sync.dma_start(
                    out=out_1[m, 7, 256 * half : 256 * half + 256].rearrange("(t j) d -> t j d", j=2), in_=r[:]
                )
